import numpy as np
import ml_dtypes


def mxq(x, axis, fmt="e4m3"):
    dtype, down = {"e4m3": (ml_dtypes.float8_e4m3fn, 7), "e5m2": (ml_dtypes.float8_e5m2, 14)}[fmt]
    v = np.moveaxis(np.asarray(x, np.float32).astype(ml_dtypes.bfloat16).astype(np.float64), axis, -1)
    blocks = v.reshape(v.shape[:-1] + (-1, 32))
    amax = np.abs(blocks).max(-1, keepdims=True)
    byte = np.maximum(np.where(amax > 0, np.frexp(amax)[1] - 1 + 127, 0) - down, 1)
    scale = np.exp2(byte - 127.0)
    codes = (blocks / scale).astype(np.float32).astype(dtype).astype(np.float64)
    return np.moveaxis((codes * scale).reshape(v.shape), -1, axis)


WIDE = False


def mx_kscale(k):
    if not WIDE:
        return np.ones(k)
    levels = np.array([10, -10, 5, -5, 0])
    a = np.random.permutation(np.resize(levels, k // 512 * 4)).reshape(k // 512, 4)
    idx = np.arange(k)
    return np.exp2(a[idx // 512, idx % 128 // 32])


BF16 = ml_dtypes.bfloat16


def bf(x):
    return np.asarray(x, np.float32).astype(BF16)


def f64(x):
    return np.asarray(x).astype(np.float64)


E2M1 = np.array([0.0, 0.5, 1.0, 1.5, 2.0, 3.0, 4.0, 6.0, -0.0, -0.5, -1.0, -1.5, -2.0, -3.0, -4.0, -6.0])


def pack_weight(w, fmt):
    k, n = w.shape
    w = f64(bf(w)).reshape(k // 32, 32, n)
    amax = np.abs(w).max(1)
    if fmt == "e4m3":
        byte = np.frexp(amax)[1] - 1 + 127 - 7
    else:
        mant, ex = np.frexp(amax / 6.0)
        byte = np.where(mant > 0.5, ex, ex - 1) + 127
    byte = np.clip(np.where(amax > 0, byte, 1), 1, 254)
    scaled = (w * np.exp2(127.0 - byte)[:, None, :]).reshape(k, n).astype(np.float32)
    by_word = np.ascontiguousarray(scaled.reshape(k // 512, 128, 4, n).transpose(0, 1, 3, 2))
    if fmt == "e4m3":
        words = by_word.astype(ml_dtypes.float8_e4m3fn).view(np.uint8)
    else:
        c = by_word.astype(ml_dtypes.float4_e2m1fn).view(np.uint8) & 0xF
        words = c[..., 0::2] | (c[..., 1::2] << 4)
    return np.ascontiguousarray(words), np.ascontiguousarray(byte.astype(np.uint8).reshape(k // 512, 16, n))


def unpack_weight(words, scales, fmt):
    g, p, n, _ = words.shape
    if fmt == "e4m3":
        vals = np.ascontiguousarray(words).view(ml_dtypes.float8_e4m3fn).astype(np.float64)
    else:
        nib = np.empty((g, p, n, 4), np.uint8)
        nib[..., 0::2] = words & 0xF
        nib[..., 1::2] = words >> 4
        vals = E2M1[nib]
    vals = vals * np.repeat(np.exp2(scales.astype(np.float64) - 127.0), 8, axis=1)[..., None]
    return vals.transpose(0, 1, 3, 2).reshape(g * 512, n)


B, S, C, H = 4, 1024, 512, 4096
WS = 1.25
FMT = "e4m3"


def setup_inputs():
    s = mx_kscale(C)
    x = bf(np.random.standard_normal((B, S, C)) * s)
    w = np.random.standard_normal((2 * C, C)) * WS / np.sqrt(C) / s[None, :]
    words, scales = pack_weight(np.ascontiguousarray(w.T), FMT)
    return {"x": x, "w_qk_words": words, "w_qk_scales": scales}


def reference(x, w_qk_words, w_qk_scales):
    qk = unpack_weight(w_qk_words, w_qk_scales, FMT).T @ mxq(f64(x), 2, "e4m3").transpose(0, 2, 1)
    q, k = qk[:, :C, :], qk[:, C:, :]
    return (mxq(q, 2, "e4m3") @ mxq(k, 2, "e4m3").transpose(0, 2, 1)) / np.sqrt(S)

@@ -1,0 +1,180 @@
+import math
+from contextlib import ExitStack
+
+import concourse.masks as masks
+import concourse.mybir as mybir
+
+F32 = mybir.dt.float32
+BF16 = mybir.dt.bfloat16
+I32 = mybir.dt.int32
+U32 = mybir.dt.uint32
+U8 = mybir.dt.uint8
+FP8X4 = mybir.dt.float8_e4m3fn_x4
+
+P = 128
+PACK = 4
+K_PASS = P * PACK
+
+BATCH = 4
+SEQ = 1024
+CH = 512
+TOKEN_PASSES = SEQ // K_PASS
+BLOCKS = CH // P
+Q_HALF = 0
+K_HALF = 1
+PSUM_BANKS = 8
+BANK_F32 = 512
+
+FLOPS = 2 * BATCH * (2 * CH) * SEQ * CH + 2 * BATCH * CH * CH * SEQ
+
+
+def tile_transformer_block_pa_t_kernel(tc, x, w_qk_words, w_qk_scales, out):
+    nc = tc.nc
+    with ExitStack() as ctx:
+        keep = ctx.enter_context(tc.tile_pool(name="keep", bufs=1))
+        stage = ctx.enter_context(tc.tile_pool(name="stage", bufs=3))
+        banks = ctx.enter_context(tc.psum_pool(name="banks", bufs=PSUM_BANKS))
+        ctx.enter_context(tc.manual_schedule())
+
+        identity = keep.tile([P, P], F32)
+        w_codes = keep.tile([P, 2 * CH], U32, align_bytes=64)
+        w_plane = keep.tile([P, 2 * CH], U8, align_bytes=64)
+        x_sb = [keep.tile([P, TOKEN_PASSES, PACK, CH], BF16, name="x_sb%d" % b) for b in range(BATCH)]
+        x_codes = [
+            keep.tile([P, TOKEN_PASSES, K_PASS], U32, name="x_codes%d" % b, align_bytes=64)
+            for b in range(BATCH)
+        ]
+        x_plane = [
+            keep.tile([P, TOKEN_PASSES, K_PASS], U8, name="x_plane%d" % b, align_bytes=64)
+            for b in range(BATCH)
+        ]
+        qk_codes = [
+            keep.tile([P, TOKEN_PASSES, 2 * CH], U32, name="qk_codes%d" % b, align_bytes=64)
+            for b in range(BATCH)
+        ]
+        qk_plane = [
+            keep.tile([P, TOKEN_PASSES, 2 * CH], U8, name="qk_plane%d" % b, align_bytes=64)
+            for b in range(BATCH)
+        ]
+
+        def load_x(b, g):
+            tokens = x[b, g * K_PASS : (g + 1) * K_PASS, :]
+            nc.sync.dma_start(out=x_sb[b][:, g], in_=tokens.rearrange("(p j) c -> p j c", j=PACK))
+
+        masks.make_identity(nc, identity[:])
+        nc.vector.memset(w_plane[:].bitcast(I32), 0)
+        load_x(0, 0)
+        for quadrant in range(4):
+            nc.sync.dma_start(
+                out=w_plane[32 * quadrant : 32 * quadrant + 4, :].bitcast(I32),
+                in_=w_qk_scales[0, 4 * quadrant : 4 * quadrant + 4, :].bitcast(I32),
+            )
+        nc.sync.dma_start(
+            out=w_codes[:].bitcast(I32),
+            in_=w_qk_words[0].rearrange("p n t -> p (n t)").bitcast(I32),
+        )
+        load_x(0, 1)
+        for b in range(1, BATCH):
+            for g in range(TOKEN_PASSES):
+                load_x(b, g)
+
+        def transpose_x(b):
+            grouped = stage.tile([P, TOKEN_PASSES, PACK, P, PACK], BF16, tag="x_grouped", align_bytes=64)
+            x_pairs = x_sb[b][:].bitcast(F32)
+            grouped_pairs = grouped[:].bitcast(F32)
+            for g in range(TOKEN_PASSES):
+                for j0 in range(0, PACK, 2):
+                    bank = banks.tile([P, 2, 2, P], F32, tag="bank")
+                    for jj in range(2):
+                        for u in range(2):
+                            nc.tensor.transpose(
+                                bank[:, jj, u, :], x_pairs[:, g, j0 + jj, u : CH // 2 : 2], identity[:]
+                            )
+                    nc.scalar.copy(
+                        out=grouped_pairs[:, g, j0 : j0 + 2],
+                        in_=bank[:].rearrange("q jj u m -> q jj m u"),
+                    )
+            return grouped
+
+        def quantise_x(b, grouped):
+            for g in range(TOKEN_PASSES):
+                nc.vector.quantize_mx(
+                    out=x_codes[b][:, g, :].bitcast(FP8X4),
+                    scales=x_plane[b][:, g, :],
+                    in_=grouped[:, g].rearrange("q j m t -> q (j m t)"),
+                )
+
+        def project(b, g, half):
+            grouped = stage.tile([P, CH, PACK], BF16, tag="qk_grouped", align_bytes=64)
+            for block in range(BLOCKS):
+                channels = slice(half * CH + block * P, half * CH + (block + 1) * P)
+                bank = banks.tile([P, PACK, P], F32, tag="bank")
+                for t in range(PACK):
+                    tokens = slice(t * P, (t + 1) * P)
+                    nc.tensor.matmul_mx(
+                        out=bank[:, t, :],
+                        lhsT=x_codes[b][:, g, tokens].bitcast(FP8X4),
+                        lhsT_scale=x_plane[b][:, g, tokens],
+                        rhs=w_codes[:, channels].bitcast(FP8X4),
+                        rhs_scale=w_plane[:, channels],
+                        start=True,
+                        stop=True,
+                    )
+                side_by_side = grouped[:, block * P : (block + 1) * P, :]
+                products = bank[:].rearrange("m t n -> m n t")
+                if block < BLOCKS - 1:
+                    nc.scalar.copy(out=side_by_side, in_=products)
+                else:
+                    nc.vector.tensor_copy(out=side_by_side, in_=products)
+            return grouped
+
+        def quantise_qk(b, g, half, grouped):
+            channels = slice(half * CH, (half + 1) * CH)
+            nc.vector.quantize_mx(
+                out=qk_codes[b][:, g, channels].bitcast(FP8X4),
+                scales=qk_plane[b][:, g, channels],
+                in_=grouped[:].rearrange("m n t -> m (n t)"),
+            )
+
+        def scores(b):
+            score_sb = stage.tile([P, BLOCKS, CH], F32, tag="score_sb")
+            k_channels = slice(CH, 2 * CH)
+            for block in range(BLOCKS):
+                q_channels = slice(block * P, (block + 1) * P)
+                bank = banks.tile([P, BANK_F32], F32, tag="bank")
+                for g in range(TOKEN_PASSES):
+                    nc.tensor.matmul_mx(
+                        out=bank[:],
+                        lhsT=qk_codes[b][:, g, q_channels].bitcast(FP8X4),
+                        lhsT_scale=qk_plane[b][:, g, q_channels],
+                        rhs=qk_codes[b][:, g, k_channels].bitcast(FP8X4),
+                        rhs_scale=qk_plane[b][:, g, k_channels],
+                        start=(g == 0),
+                        stop=(g == TOKEN_PASSES - 1),
+                    )
+                nc.vector.tensor_scalar_mul(
+                    out=score_sb[:, block, :], in0=bank[:], scalar1=1.0 / math.sqrt(SEQ)
+                )
+                nc.sync.dma_start(out=out[b, q_channels, :], in_=score_sb[:, block, :])
+
+        x_grouped = transpose_x(0)
+        quantise_x(0, x_grouped)
+        last = None
+        for b in range(BATCH):
+            q0 = project(b, 0, Q_HALF)
+            if b > 0:
+                quantise_qk(b - 1, 1, K_HALF, last)
+            if b + 1 < BATCH:
+                x_grouped = transpose_x(b + 1)
+            k0 = project(b, 0, K_HALF)
+            quantise_qk(b, 0, Q_HALF, q0)
+            if b + 1 < BATCH:
+                quantise_x(b + 1, x_grouped)
+            if b > 0:
+                scores(b - 1)
+            q1 = project(b, 1, Q_HALF)
+            quantise_qk(b, 0, K_HALF, k0)
+            last = project(b, 1, K_HALF)
+            quantise_qk(b, 1, Q_HALF, q1)
+        quantise_qk(BATCH - 1, 1, K_HALF, last)
+        scores(BATCH - 1)

@@ -20,10 +20,14 @@ SEQ = 1024
 CH = 512
 TOKEN_PASSES = SEQ // K_PASS
 BLOCKS = CH // P
-Q_HALF = 0
-K_HALF = 1
 PSUM_BANKS = 8
 BANK_F32 = 512
+
+K_PAIRS = 4
+Q_PAIRS = 4
+PAIRS = K_PAIRS + Q_PAIRS
+STEPS = BATCH * PAIRS
+SCORE_LAG = 2
 
 FLOPS = 2 * BATCH * (2 * CH) * SEQ * CH + 2 * BATCH * CH * CH * SEQ
 
@@ -32,11 +36,12 @@ def tile_transformer_block_pa_t_kernel(tc, x, w_qk_words, w_qk_scales, out):
     nc = tc.nc
     with ExitStack() as ctx:
         keep = ctx.enter_context(tc.tile_pool(name="keep", bufs=1))
-        stage = ctx.enter_context(tc.tile_pool(name="stage", bufs=3))
+        stage = ctx.enter_context(tc.tile_pool(name="stage", bufs=4))
         banks = ctx.enter_context(tc.psum_pool(name="banks", bufs=PSUM_BANKS))
         ctx.enter_context(tc.manual_schedule())
 
         identity = keep.tile([P, P], F32)
+        table_warmer = keep.tile([P, 1], F32)
         w_codes = keep.tile([P, 2 * CH], U32, align_bytes=64)
         w_plane = keep.tile([P, 2 * CH], U8, align_bytes=64)
         x_sb = [keep.tile([P, TOKEN_PASSES, PACK, CH], BF16, name="x_sb%d" % b) for b in range(BATCH)]
@@ -48,22 +53,32 @@ def tile_transformer_block_pa_t_kernel(tc, x, w_qk_words, w_qk_scales, out):
             keep.tile([P, TOKEN_PASSES, K_PASS], U8, name="x_plane%d" % b, align_bytes=64)
             for b in range(BATCH)
         ]
-        qk_codes = [
-            keep.tile([P, TOKEN_PASSES, 2 * CH], U32, name="qk_codes%d" % b, align_bytes=64)
+        k_codes = [
+            keep.tile([P, TOKEN_PASSES, CH], U32, name="k_codes%d" % b, align_bytes=64)
             for b in range(BATCH)
         ]
-        qk_plane = [
-            keep.tile([P, TOKEN_PASSES, 2 * CH], U8, name="qk_plane%d" % b, align_bytes=64)
+        k_plane = [
+            keep.tile([P, TOKEN_PASSES, CH], U8, name="k_plane%d" % b, align_bytes=64)
+            for b in range(BATCH)
+        ]
+        q_codes = [
+            keep.tile([P, BLOCKS, TOKEN_PASSES, P], U32, name="q_codes%d" % b, align_bytes=64)
+            for b in range(BATCH)
+        ]
+        q_plane = [
+            keep.tile([P, BLOCKS, TOKEN_PASSES, P], U8, name="q_plane%d" % b, align_bytes=64)
             for b in range(BATCH)
         ]
 
         def load_x(b, g):
-            tokens = x[b, g * K_PASS : (g + 1) * K_PASS, :]
-            nc.sync.dma_start(out=x_sb[b][:, g], in_=tokens.rearrange("(p j) c -> p j c", j=PACK))
+            rows = x[b, g * K_PASS : (g + 1) * K_PASS, :]
+            nc.sync.dma_start(out=x_sb[b][:, g], in_=rows.rearrange("(p j) c -> p j c", j=PACK))
 
         masks.make_identity(nc, identity[:])
         nc.vector.memset(w_plane[:].bitcast(I32), 0)
+        nc.scalar.mul(out=table_warmer[:], in_=identity[:, 0:1], mul=1.0)
         load_x(0, 0)
+        load_x(0, 1)
         for quadrant in range(4):
             nc.sync.dma_start(
                 out=w_plane[32 * quadrant : 32 * quadrant + 4, :].bitcast(I32),
@@ -73,13 +88,12 @@ def tile_transformer_block_pa_t_kernel(tc, x, w_qk_words, w_qk_scales, out):
             out=w_codes[:].bitcast(I32),
             in_=w_qk_words[0].rearrange("p n t -> p (n t)").bitcast(I32),
         )
-        load_x(0, 1)
         for b in range(1, BATCH):
             for g in range(TOKEN_PASSES):
                 load_x(b, g)
 
         def transpose_x(b):
-            grouped = stage.tile([P, TOKEN_PASSES, PACK, P, PACK], BF16, tag="x_grouped", align_bytes=64)
+            grouped = stage.tile([P, TOKEN_PASSES, PACK, P, PACK], BF16, tag="x_grouped", bufs=2, align_bytes=64)
             x_pairs = x_sb[b][:].bitcast(F32)
             grouped_pairs = grouped[:].bitcast(F32)
             for g in range(TOKEN_PASSES):
@@ -96,18 +110,21 @@ def tile_transformer_block_pa_t_kernel(tc, x, w_qk_words, w_qk_scales, out):
                     )
             return grouped
 
-        def quantise_x(b, grouped):
-            for g in range(TOKEN_PASSES):
-                nc.vector.quantize_mx(
-                    out=x_codes[b][:, g, :].bitcast(FP8X4),
-                    scales=x_plane[b][:, g, :],
-                    in_=grouped[:, g].rearrange("q j m t -> q (j m t)"),
-                )
+        def quantise_x(b, g, grouped):
+            nc.vector.quantize_mx(
+                out=x_codes[b][:, g, :].bitcast(FP8X4),
+                scales=x_plane[b][:, g, :],
+                in_=grouped[:, g].rearrange("q j m t -> q (j m t)"),
+            )
 
-        def project(b, g, half):
-            grouped = stage.tile([P, CH, PACK], BF16, tag="qk_grouped", align_bytes=64)
-            for block in range(BLOCKS):
-                channels = slice(half * CH + block * P, half * CH + (block + 1) * P)
+        def project_pair(b, r):
+            grouped = stage.tile([P, 2, P, PACK], BF16, tag="qk_grouped", align_bytes=64)
+            for i in range(2):
+                if r < K_PAIRS:
+                    g, w_block = r // 2, BLOCKS + 2 * (r % 2) + i
+                else:
+                    g, w_block = i, r - K_PAIRS
+                channels = slice(w_block * P, (w_block + 1) * P)
                 bank = banks.tile([P, PACK, P], F32, tag="bank")
                 for t in range(PACK):
                     tokens = slice(t * P, (t + 1) * P)
@@ -120,61 +137,57 @@ def tile_transformer_block_pa_t_kernel(tc, x, w_qk_words, w_qk_scales, out):
                         start=True,
                         stop=True,
                     )
-                side_by_side = grouped[:, block * P : (block + 1) * P, :]
                 products = bank[:].rearrange("m t n -> m n t")
-                if block < BLOCKS - 1:
-                    nc.scalar.copy(out=side_by_side, in_=products)
+                if i == 0:
+                    nc.scalar.copy(out=grouped[:, i], in_=products)
                 else:
-                    nc.vector.tensor_copy(out=side_by_side, in_=products)
+                    nc.vector.tensor_copy(out=grouped[:, i], in_=products)
             return grouped
 
-        def quantise_qk(b, g, half, grouped):
-            channels = slice(half * CH, (half + 1) * CH)
+        def quantise_pair(b, r, grouped):
+            if r < K_PAIRS:
+                channels = slice(2 * P * (r % 2), 2 * P * (r % 2 + 1))
+                codes = k_codes[b][:, r // 2, channels]
+                plane = k_plane[b][:, r // 2, channels]
+            else:
+                codes = q_codes[b][:, r - K_PAIRS].rearrange("m g n -> m (g n)")
+                plane = q_plane[b][:, r - K_PAIRS].rearrange("m g n -> m (g n)")
             nc.vector.quantize_mx(
-                out=qk_codes[b][:, g, channels].bitcast(FP8X4),
-                scales=qk_plane[b][:, g, channels],
-                in_=grouped[:].rearrange("m n t -> m (n t)"),
+                out=codes.bitcast(FP8X4),
+                scales=plane,
+                in_=grouped[:].rearrange("m i n t -> m (i n t)"),
             )
 
-        def scores(b):
-            score_sb = stage.tile([P, BLOCKS, CH], F32, tag="score_sb")
-            k_channels = slice(CH, 2 * CH)
-            for block in range(BLOCKS):
-                q_channels = slice(block * P, (block + 1) * P)
-                bank = banks.tile([P, BANK_F32], F32, tag="bank")
-                for g in range(TOKEN_PASSES):
-                    nc.tensor.matmul_mx(
-                        out=bank[:],
-                        lhsT=qk_codes[b][:, g, q_channels].bitcast(FP8X4),
-                        lhsT_scale=qk_plane[b][:, g, q_channels],
-                        rhs=qk_codes[b][:, g, k_channels].bitcast(FP8X4),
-                        rhs_scale=qk_plane[b][:, g, k_channels],
-                        start=(g == 0),
-                        stop=(g == TOKEN_PASSES - 1),
-                    )
-                nc.vector.tensor_scalar_mul(
-                    out=score_sb[:, block, :], in0=bank[:], scalar1=1.0 / math.sqrt(SEQ)
+        def scores(b, block):
+            bank = banks.tile([P, BANK_F32], F32, tag="bank")
+            for g in range(TOKEN_PASSES):
+                nc.tensor.matmul_mx(
+                    out=bank[:],
+                    lhsT=q_codes[b][:, block, g, :].bitcast(FP8X4),
+                    lhsT_scale=q_plane[b][:, block, g, :],
+                    rhs=k_codes[b][:, g, :].bitcast(FP8X4),
+                    rhs_scale=k_plane[b][:, g, :],
+                    start=(g == 0),
+                    stop=(g == TOKEN_PASSES - 1),
                 )
-                nc.sync.dma_start(out=out[b, q_channels, :], in_=score_sb[:, block, :])
+            score_sb = stage.tile([P, CH], F32, tag="score_sb")
+            nc.scalar.mul(out=score_sb[:], in_=bank[:], mul=1.0 / math.sqrt(SEQ))
+            nc.sync.dma_start(out=out[b, block * P : (block + 1) * P, :], in_=score_sb[:])
 
         x_grouped = transpose_x(0)
-        quantise_x(0, x_grouped)
-        last = None
-        for b in range(BATCH):
-            q0 = project(b, 0, Q_HALF)
-            if b > 0:
-                quantise_qk(b - 1, 1, K_HALF, last)
-            if b + 1 < BATCH:
-                x_grouped = transpose_x(b + 1)
-            k0 = project(b, 0, K_HALF)
-            quantise_qk(b, 0, Q_HALF, q0)
-            if b + 1 < BATCH:
-                quantise_x(b + 1, x_grouped)
-            if b > 0:
-                scores(b - 1)
-            q1 = project(b, 1, Q_HALF)
-            quantise_qk(b, 0, K_HALF, k0)
-            last = project(b, 1, K_HALF)
-            quantise_qk(b, 1, Q_HALF, q1)
-        quantise_qk(BATCH - 1, 1, K_HALF, last)
-        scores(BATCH - 1)
+        quantise_x(0, 0, x_grouped)
+        quantise_x(0, 1, x_grouped)
+        qk_grouped = None
+        for step in range(STEPS + SCORE_LAG):
+            b, r = divmod(step, PAIRS)
+            if 1 <= step <= STEPS:
+                quantise_pair((step - 1) // PAIRS, (step - 1) % PAIRS, qk_grouped)
+            if step < STEPS:
+                qk_grouped = project_pair(b, r)
+                if b + 1 < BATCH and r == K_PAIRS - 1:
+                    x_grouped = transpose_x(b + 1)
+                    quantise_x(b + 1, 0, x_grouped)
+                if b + 1 < BATCH and r == K_PAIRS:
+                    quantise_x(b + 1, 1, x_grouped)
+            if step >= SCORE_LAG and (step - SCORE_LAG) % PAIRS >= K_PAIRS:
+                scores((step - SCORE_LAG) // PAIRS, (step - SCORE_LAG) % PAIRS - K_PAIRS)

@@ -23,12 +23,6 @@ BLOCKS = CH // P
 PSUM_BANKS = 8
 BANK_F32 = 512
 
-K_PAIRS = 4
-Q_PAIRS = 4
-PAIRS = K_PAIRS + Q_PAIRS
-STEPS = BATCH * PAIRS
-SCORE_LAG = 2
-
 FLOPS = 2 * BATCH * (2 * CH) * SEQ * CH + 2 * BATCH * CH * CH * SEQ
 
 
@@ -40,39 +34,26 @@ def tile_transformer_block_pa_t_kernel(tc, x, w_qk_words, w_qk_scales, out):
         banks = ctx.enter_context(tc.psum_pool(name="banks", bufs=PSUM_BANKS))
         ctx.enter_context(tc.manual_schedule())
 
+        batch_passes = [(b, g) for b in range(BATCH) for g in range(TOKEN_PASSES)]
         identity = keep.tile([P, P], F32)
         table_warmer = keep.tile([P, 1], F32)
         w_codes = keep.tile([P, 2 * CH], U32, align_bytes=64)
         w_plane = keep.tile([P, 2 * CH], U8, align_bytes=64)
-        x_sb = [keep.tile([P, TOKEN_PASSES, PACK, CH], BF16, name="x_sb%d" % b) for b in range(BATCH)]
-        x_codes = [
-            keep.tile([P, TOKEN_PASSES, K_PASS], U32, name="x_codes%d" % b, align_bytes=64)
-            for b in range(BATCH)
-        ]
-        x_plane = [
-            keep.tile([P, TOKEN_PASSES, K_PASS], U8, name="x_plane%d" % b, align_bytes=64)
-            for b in range(BATCH)
-        ]
-        k_codes = [
-            keep.tile([P, TOKEN_PASSES, CH], U32, name="k_codes%d" % b, align_bytes=64)
-            for b in range(BATCH)
-        ]
-        k_plane = [
-            keep.tile([P, TOKEN_PASSES, CH], U8, name="k_plane%d" % b, align_bytes=64)
-            for b in range(BATCH)
-        ]
-        q_codes = [
-            keep.tile([P, BLOCKS, TOKEN_PASSES, P], U32, name="q_codes%d" % b, align_bytes=64)
-            for b in range(BATCH)
-        ]
-        q_plane = [
-            keep.tile([P, BLOCKS, TOKEN_PASSES, P], U8, name="q_plane%d" % b, align_bytes=64)
-            for b in range(BATCH)
-        ]
+        x_sb = {}
+        x_codes = {}
+        x_plane = {}
+        qk_codes = {}
+        qk_plane = {}
+        for b, g in batch_passes:
+            x_sb[b, g] = keep.tile([P, PACK, CH], BF16, name="x_sb%d%d" % (b, g))
+            x_codes[b, g] = keep.tile([P, K_PASS], U32, name="x_codes%d%d" % (b, g), align_bytes=64)
+            x_plane[b, g] = keep.tile([P, K_PASS], U8, name="x_plane%d%d" % (b, g), align_bytes=64)
+            qk_codes[b, g] = keep.tile([P, 2 * CH], U32, name="qk_codes%d%d" % (b, g), align_bytes=64)
+            qk_plane[b, g] = keep.tile([P, 2 * CH], U8, name="qk_plane%d%d" % (b, g), align_bytes=64)
 
         def load_x(b, g):
             rows = x[b, g * K_PASS : (g + 1) * K_PASS, :]
-            nc.sync.dma_start(out=x_sb[b][:, g], in_=rows.rearrange("(p j) c -> p j c", j=PACK))
+            nc.sync.dma_start(out=x_sb[b, g][:], in_=rows.rearrange("(p j) c -> p j c", j=PACK))
 
         masks.make_identity(nc, identity[:])
         nc.vector.memset(w_plane[:].bitcast(I32), 0)
@@ -88,106 +69,113 @@ def tile_transformer_block_pa_t_kernel(tc, x, w_qk_words, w_qk_scales, out):
             out=w_codes[:].bitcast(I32),
             in_=w_qk_words[0].rearrange("p n t -> p (n t)").bitcast(I32),
         )
-        for b in range(1, BATCH):
-            for g in range(TOKEN_PASSES):
-                load_x(b, g)
+        for b, g in batch_passes[TOKEN_PASSES:]:
+            load_x(b, g)
 
-        def transpose_x(b):
-            grouped = stage.tile([P, TOKEN_PASSES, PACK, P, PACK], BF16, tag="x_grouped", bufs=2, align_bytes=64)
-            x_pairs = x_sb[b][:].bitcast(F32)
-            grouped_pairs = grouped[:].bitcast(F32)
-            for g in range(TOKEN_PASSES):
-                for j0 in range(0, PACK, 2):
-                    bank = banks.tile([P, 2, 2, P], F32, tag="bank")
-                    for jj in range(2):
-                        for u in range(2):
-                            nc.tensor.transpose(
-                                bank[:, jj, u, :], x_pairs[:, g, j0 + jj, u : CH // 2 : 2], identity[:]
-                            )
-                    nc.scalar.copy(
-                        out=grouped_pairs[:, g, j0 : j0 + 2],
-                        in_=bank[:].rearrange("q jj u m -> q jj m u"),
-                    )
-            return grouped
-
-        def quantise_x(b, g, grouped):
-            nc.vector.quantize_mx(
-                out=x_codes[b][:, g, :].bitcast(FP8X4),
-                scales=x_plane[b][:, g, :],
-                in_=grouped[:, g].rearrange("q j m t -> q (j m t)"),
-            )
-
-        def project_pair(b, r):
-            grouped = stage.tile([P, 2, P, PACK], BF16, tag="qk_grouped", align_bytes=64)
-            for i in range(2):
-                if r < K_PAIRS:
-                    g, w_block = r // 2, BLOCKS + 2 * (r % 2) + i
-                else:
-                    g, w_block = i, r - K_PAIRS
-                channels = slice(w_block * P, (w_block + 1) * P)
-                bank = banks.tile([P, PACK, P], F32, tag="bank")
-                for t in range(PACK):
-                    tokens = slice(t * P, (t + 1) * P)
-                    nc.tensor.matmul_mx(
-                        out=bank[:, t, :],
-                        lhsT=x_codes[b][:, g, tokens].bitcast(FP8X4),
-                        lhsT_scale=x_plane[b][:, g, tokens],
-                        rhs=w_codes[:, channels].bitcast(FP8X4),
-                        rhs_scale=w_plane[:, channels],
-                        start=True,
-                        stop=True,
-                    )
-                products = bank[:].rearrange("m t n -> m n t")
-                if i == 0:
-                    nc.scalar.copy(out=grouped[:, i], in_=products)
-                else:
-                    nc.vector.tensor_copy(out=grouped[:, i], in_=products)
-            return grouped
-
-        def quantise_pair(b, r, grouped):
-            if r < K_PAIRS:
-                channels = slice(2 * P * (r % 2), 2 * P * (r % 2 + 1))
-                codes = k_codes[b][:, r // 2, channels]
-                plane = k_plane[b][:, r // 2, channels]
-            else:
-                codes = q_codes[b][:, r - K_PAIRS].rearrange("m g n -> m (g n)")
-                plane = q_plane[b][:, r - K_PAIRS].rearrange("m g n -> m (g n)")
-            nc.vector.quantize_mx(
-                out=codes.bitcast(FP8X4),
-                scales=plane,
-                in_=grouped[:].rearrange("m i n t -> m (i n t)"),
-            )
-
-        def scores(b, block):
-            bank = banks.tile([P, BANK_F32], F32, tag="bank")
-            for g in range(TOKEN_PASSES):
-                nc.tensor.matmul_mx(
-                    out=bank[:],
-                    lhsT=q_codes[b][:, block, g, :].bitcast(FP8X4),
-                    lhsT_scale=q_plane[b][:, block, g, :],
-                    rhs=k_codes[b][:, g, :].bitcast(FP8X4),
-                    rhs_scale=k_plane[b][:, g, :],
-                    start=(g == 0),
-                    stop=(g == TOKEN_PASSES - 1),
+        def transpose_x(b, g):
+            x_grouped = stage.tile([P, PACK, P, PACK], BF16, tag="x_grouped", align_bytes=64)
+            x_pairs = x_sb[b, g][:].bitcast(F32)
+            grouped_pairs = x_grouped[:].bitcast(F32)
+            for j0 in range(0, PACK, 2):
+                bank = banks.tile([P, 2, 2, P], F32, tag="bank")
+                for jj in range(2):
+                    for u in range(2):
+                        nc.tensor.transpose(
+                            bank[:, jj, u, :], x_pairs[:, j0 + jj, u : CH // 2 : 2], identity[:]
+                        )
+                nc.scalar.copy(
+                    out=grouped_pairs[:, j0 : j0 + 2],
+                    in_=bank[:].rearrange("q jj u m -> q jj m u"),
                 )
-            score_sb = stage.tile([P, CH], F32, tag="score_sb")
-            nc.scalar.mul(out=score_sb[:], in_=bank[:], mul=1.0 / math.sqrt(SEQ))
-            nc.sync.dma_start(out=out[b, block * P : (block + 1) * P, :], in_=score_sb[:])
+            return x_grouped
 
-        x_grouped = transpose_x(0)
-        quantise_x(0, 0, x_grouped)
-        quantise_x(0, 1, x_grouped)
-        qk_grouped = None
-        for step in range(STEPS + SCORE_LAG):
-            b, r = divmod(step, PAIRS)
-            if 1 <= step <= STEPS:
-                quantise_pair((step - 1) // PAIRS, (step - 1) % PAIRS, qk_grouped)
-            if step < STEPS:
-                qk_grouped = project_pair(b, r)
-                if b + 1 < BATCH and r == K_PAIRS - 1:
-                    x_grouped = transpose_x(b + 1)
-                    quantise_x(b + 1, 0, x_grouped)
-                if b + 1 < BATCH and r == K_PAIRS:
-                    quantise_x(b + 1, 1, x_grouped)
-            if step >= SCORE_LAG and (step - SCORE_LAG) % PAIRS >= K_PAIRS:
-                scores((step - SCORE_LAG) // PAIRS, (step - SCORE_LAG) % PAIRS - K_PAIRS)
+        def quantise_x(b, g, x_grouped):
+            nc.vector.quantize_mx(
+                out=x_codes[b, g][:].bitcast(FP8X4),
+                scales=x_plane[b, g][:],
+                in_=x_grouped[:].rearrange("q j m t -> q (j m t)"),
+            )
+
+        def project_block(b, g, block, side_by_side, copy_out):
+            channels = slice(block * P, (block + 1) * P)
+            bank = banks.tile([P, PACK, P], F32, tag="bank")
+            for t in range(PACK):
+                tokens = slice(t * P, (t + 1) * P)
+                nc.tensor.matmul_mx(
+                    out=bank[:, t, :],
+                    lhsT=x_codes[b, g][:, tokens].bitcast(FP8X4),
+                    lhsT_scale=x_plane[b, g][:, tokens],
+                    rhs=w_codes[:, channels].bitcast(FP8X4),
+                    rhs_scale=w_plane[:, channels],
+                    start=True,
+                    stop=True,
+                )
+            copy_out(out=side_by_side, in_=bank[:].rearrange("m t n -> m n t"))
+
+        def project(b, g):
+            grouped_tiles = []
+            for first_block in range(0, 2 * BLOCKS, 4):
+                by_scalar = stage.tile([P, 2, P, PACK], BF16, tag="by_scalar", align_bytes=64)
+                by_vector = stage.tile([P, 2, P, PACK], BF16, tag="by_vector", align_bytes=64)
+                for i in range(2):
+                    project_block(b, g, first_block + i, by_scalar[:, i], nc.scalar.copy)
+                    project_block(b, g, first_block + 2 + i, by_vector[:, i], nc.vector.tensor_copy)
+                grouped_tiles.extend([by_scalar, by_vector])
+            return grouped_tiles
+
+        def quantise_qk(b, g, grouped_tiles):
+            for n, grouped in enumerate(grouped_tiles):
+                channels = slice(n * 2 * P, (n + 1) * 2 * P)
+                nc.vector.quantize_mx(
+                    out=qk_codes[b, g][:, channels].bitcast(FP8X4),
+                    scales=qk_plane[b, g][:, channels],
+                    in_=grouped[:].rearrange("m i n t -> m (i n t)"),
+                )
+
+        def scores(b):
+            score_banks = [
+                banks.tile([P, BANK_F32], F32, tag="bank", name="score_bank%d" % block)
+                for block in range(BLOCKS)
+            ]
+            for g in range(TOKEN_PASSES):
+                for block in range(BLOCKS):
+                    q_channels = slice(block * P, (block + 1) * P)
+                    nc.tensor.matmul_mx(
+                        out=score_banks[block][:],
+                        lhsT=qk_codes[b, g][:, q_channels].bitcast(FP8X4),
+                        lhsT_scale=qk_plane[b, g][:, q_channels],
+                        rhs=qk_codes[b, g][:, CH : 2 * CH].bitcast(FP8X4),
+                        rhs_scale=qk_plane[b, g][:, CH : 2 * CH],
+                        start=(g == 0),
+                        stop=(g == TOKEN_PASSES - 1),
+                    )
+            for block in range(BLOCKS):
+                score_sb = stage.tile([P, CH], F32, tag="score_sb")
+                if block < BLOCKS - 1:
+                    nc.scalar.mul(out=score_sb[:], in_=score_banks[block][:], mul=1.0 / math.sqrt(SEQ))
+                else:
+                    nc.vector.tensor_scalar_mul(
+                        out=score_sb[:], in0=score_banks[block][:], scalar1=1.0 / math.sqrt(SEQ)
+                    )
+                nc.sync.dma_start(out=out[b, block * P : (block + 1) * P, :], in_=score_sb[:])
+
+        x_grouped_0 = transpose_x(0, 0)
+        x_grouped_1 = transpose_x(0, 1)
+        quantise_x(0, 0, x_grouped_0)
+        quantise_x(0, 1, x_grouped_1)
+        for b in range(BATCH):
+            more = b + 1 < BATCH
+            grouped_tiles = project(b, 0)
+            if more:
+                x_grouped_0 = transpose_x(b + 1, 0)
+                x_grouped_1 = transpose_x(b + 1, 1)
+            quantise_qk(b, 0, grouped_tiles)
+            if more:
+                quantise_x(b + 1, 0, x_grouped_0)
+            grouped_tiles = project(b, 1)
+            if more:
+                quantise_x(b + 1, 1, x_grouped_1)
+            quantise_qk(b, 1, grouped_tiles)
+            if b > 0:
+                scores(b - 1)
+        scores(BATCH - 1)

@@ -52,8 +52,9 @@ def tile_transformer_block_pa_t_kernel(tc, x, w_qk_words, w_qk_scales, out):
             qk_plane[b, g] = keep.tile([P, 2 * CH], U8, name="qk_plane%d%d" % (b, g), align_bytes=64)
 
         def load_x(b, g):
-            rows = x[b, g * K_PASS : (g + 1) * K_PASS, :]
-            nc.sync.dma_start(out=x_sb[b, g][:], in_=rows.rearrange("(p j) c -> p j c", j=PACK))
+            rows = x[b, g * K_PASS : (g + 1) * K_PASS, :].rearrange("(p j) c -> p j c", j=PACK)
+            for j0 in range(0, PACK, 2):
+                nc.sync.dma_start(out=x_sb[b, g][:, j0 : j0 + 2], in_=rows[:, j0 : j0 + 2])
 
         masks.make_identity(nc, identity[:])
         nc.vector.memset(w_plane[:].bitcast(I32), 0)
@@ -65,10 +66,9 @@ def tile_transformer_block_pa_t_kernel(tc, x, w_qk_words, w_qk_scales, out):
                 out=w_plane[32 * quadrant : 32 * quadrant + 4, :].bitcast(I32),
                 in_=w_qk_scales[0, 4 * quadrant : 4 * quadrant + 4, :].bitcast(I32),
             )
-        nc.sync.dma_start(
-            out=w_codes[:].bitcast(I32),
-            in_=w_qk_words[0].rearrange("p n t -> p (n t)").bitcast(I32),
-        )
+        w_words = w_qk_words[0].rearrange("p n t -> p (n t)").bitcast(I32)
+        for channels in (slice(0, CH), slice(CH, 2 * CH)):
+            nc.sync.dma_start(out=w_codes[:, channels].bitcast(I32), in_=w_words[:, channels])
         for b, g in batch_passes[TOKEN_PASSES:]:
             load_x(b, g)
 
@@ -150,7 +150,7 @@ def tile_transformer_block_pa_t_kernel(tc, x, w_qk_words, w_qk_scales, out):
                         stop=(g == TOKEN_PASSES - 1),
                     )
             for block in range(BLOCKS):
-                score_sb = stage.tile([P, CH], F32, tag="score_sb")
+                score_sb = stage.tile([P, CH], F32, tag="score_sb", bufs=2 * BLOCKS)
                 if block < BLOCKS - 1:
                     nc.scalar.mul(out=score_sb[:], in_=score_banks[block][:], mul=1.0 / math.sqrt(SEQ))
                 else:

@@ -36,7 +36,6 @@ def tile_transformer_block_pa_t_kernel(tc, x, w_qk_words, w_qk_scales, out):
 
         batch_passes = [(b, g) for b in range(BATCH) for g in range(TOKEN_PASSES)]
         identity = keep.tile([P, P], F32)
-        table_warmer = keep.tile([P, 1], F32)
         w_codes = keep.tile([P, 2 * CH], U32, align_bytes=64)
         w_plane = keep.tile([P, 2 * CH], U8, align_bytes=64)
         x_sb = {}
@@ -58,7 +57,6 @@ def tile_transformer_block_pa_t_kernel(tc, x, w_qk_words, w_qk_scales, out):
 
         masks.make_identity(nc, identity[:])
         nc.vector.memset(w_plane[:].bitcast(I32), 0)
-        nc.scalar.mul(out=table_warmer[:], in_=identity[:, 0:1], mul=1.0)
         load_x(0, 0)
         load_x(0, 1)
         for quadrant in range(4):

@@ -87,12 +87,15 @@ def tile_transformer_block_pa_t_kernel(tc, x, w_qk_words, w_qk_scales, out):
                 )
             return x_grouped
 
-        def quantise_x(b, g, x_grouped):
-            nc.vector.quantize_mx(
-                out=x_codes[b, g][:].bitcast(FP8X4),
-                scales=x_plane[b, g][:],
-                in_=x_grouped[:].rearrange("q j m t -> q (j m t)"),
-            )
+        def quantise_x(b, g, x_grouped, parts=1):
+            width = PACK // parts
+            for j0 in range(0, PACK, width):
+                columns = slice(j0 * P, (j0 + width) * P)
+                nc.vector.quantize_mx(
+                    out=x_codes[b, g][:, columns].bitcast(FP8X4),
+                    scales=x_plane[b, g][:, columns],
+                    in_=x_grouped[:, j0 : j0 + width].rearrange("q j m t -> q (j m t)"),
+                )
 
         def project_block(b, g, block, side_by_side, copy_out):
             channels = slice(block * P, (block + 1) * P)
@@ -110,56 +113,88 @@ def tile_transformer_block_pa_t_kernel(tc, x, w_qk_words, w_qk_scales, out):
                 )
             copy_out(out=side_by_side, in_=bank[:].rearrange("m t n -> m n t"))
 
+        def project_half(b, g, first_block):
+            by_scalar = stage.tile([P, 2, P, PACK], BF16, tag="by_scalar", align_bytes=64)
+            by_vector = stage.tile([P, 2, P, PACK], BF16, tag="by_vector", align_bytes=64)
+            for i in range(2):
+                project_block(b, g, first_block + i, by_scalar[:, i], nc.scalar.copy)
+                project_block(b, g, first_block + 2 + i, by_vector[:, i], nc.vector.tensor_copy)
+            return [(first_block, by_scalar), (first_block + 2, by_vector)]
+
         def project(b, g):
-            grouped_tiles = []
-            for first_block in range(0, 2 * BLOCKS, 4):
-                by_scalar = stage.tile([P, 2, P, PACK], BF16, tag="by_scalar", align_bytes=64)
-                by_vector = stage.tile([P, 2, P, PACK], BF16, tag="by_vector", align_bytes=64)
-                for i in range(2):
-                    project_block(b, g, first_block + i, by_scalar[:, i], nc.scalar.copy)
-                    project_block(b, g, first_block + 2 + i, by_vector[:, i], nc.vector.tensor_copy)
-                grouped_tiles.extend([by_scalar, by_vector])
-            return grouped_tiles
+            return project_half(b, g, 0) + project_half(b, g, BLOCKS)
 
         def quantise_qk(b, g, grouped_tiles):
-            for n, grouped in enumerate(grouped_tiles):
-                channels = slice(n * 2 * P, (n + 1) * 2 * P)
+            for first_block, grouped in grouped_tiles:
+                channels = slice(first_block * P, (first_block + grouped.shape[1]) * P)
                 nc.vector.quantize_mx(
                     out=qk_codes[b, g][:, channels].bitcast(FP8X4),
                     scales=qk_plane[b, g][:, channels],
                     in_=grouped[:].rearrange("m i n t -> m (i n t)"),
                 )
 
+        def last_project(b, g):
+            quantise_qk(b, g, project_half(b, g, BLOCKS))
+            q_01 = stage.tile([P, 2, P, PACK], BF16, tag="by_scalar", align_bytes=64)
+            q_2 = stage.tile([P, 1, P, PACK], BF16, tag="by_vector", align_bytes=64)
+            q_3 = stage.tile([P, 1, P, PACK], BF16, tag="by_scalar", align_bytes=64)
+            project_block(b, g, 0, q_01[:, 0], nc.scalar.copy)
+            project_block(b, g, 2, q_2[:, 0], nc.vector.tensor_copy)
+            project_block(b, g, 1, q_01[:, 1], nc.scalar.copy)
+            project_block(b, g, 3, q_3[:, 0], nc.scalar.copy)
+            quantise_qk(b, g, [(0, q_01), (2, q_2), (3, q_3)])
+
+        def score_pass(bank, b, g, block, columns):
+            q_channels = slice(block * P, (block + 1) * P)
+            k_channels = slice(CH + columns.start, CH + columns.stop)
+            nc.tensor.matmul_mx(
+                out=bank[:, : columns.stop - columns.start],
+                lhsT=qk_codes[b, g][:, q_channels].bitcast(FP8X4),
+                lhsT_scale=qk_plane[b, g][:, q_channels],
+                rhs=qk_codes[b, g][:, k_channels].bitcast(FP8X4),
+                rhs_scale=qk_plane[b, g][:, k_channels],
+                start=(g == 0),
+                stop=(g == TOKEN_PASSES - 1),
+            )
+
+        def store_scores(bank, b, block, columns, by_vector):
+            width = columns.stop - columns.start
+            score_sb = stage.tile([P, CH], F32, tag="score_sb", bufs=2 * BLOCKS)
+            if by_vector:
+                nc.vector.tensor_scalar_mul(
+                    out=score_sb[:, :width], in0=bank[:, :width], scalar1=1.0 / math.sqrt(SEQ)
+                )
+            else:
+                nc.scalar.mul(out=score_sb[:, :width], in_=bank[:, :width], mul=1.0 / math.sqrt(SEQ))
+            nc.sync.dma_start(
+                out=out[b, block * P : (block + 1) * P, columns], in_=score_sb[:, :width]
+            )
+
         def scores(b):
+            columns = slice(0, CH)
             score_banks = [
                 banks.tile([P, BANK_F32], F32, tag="bank", name="score_bank%d" % block)
                 for block in range(BLOCKS)
             ]
             for g in range(TOKEN_PASSES):
                 for block in range(BLOCKS):
-                    q_channels = slice(block * P, (block + 1) * P)
-                    nc.tensor.matmul_mx(
-                        out=score_banks[block][:],
-                        lhsT=qk_codes[b, g][:, q_channels].bitcast(FP8X4),
-                        lhsT_scale=qk_plane[b, g][:, q_channels],
-                        rhs=qk_codes[b, g][:, CH : 2 * CH].bitcast(FP8X4),
-                        rhs_scale=qk_plane[b, g][:, CH : 2 * CH],
-                        start=(g == 0),
-                        stop=(g == TOKEN_PASSES - 1),
-                    )
+                    score_pass(score_banks[block], b, g, block, columns)
             for block in range(BLOCKS):
-                score_sb = stage.tile([P, CH], F32, tag="score_sb", bufs=2 * BLOCKS)
-                if block < BLOCKS - 1:
-                    nc.scalar.mul(out=score_sb[:], in_=score_banks[block][:], mul=1.0 / math.sqrt(SEQ))
-                else:
-                    nc.vector.tensor_scalar_mul(
-                        out=score_sb[:], in0=score_banks[block][:], scalar1=1.0 / math.sqrt(SEQ)
-                    )
-                nc.sync.dma_start(out=out[b, block * P : (block + 1) * P, :], in_=score_sb[:])
+                store_scores(score_banks[block], b, block, columns, by_vector=(block == BLOCKS - 1))
+
+        def last_scores(b):
+            halves = [slice(0, CH // 2), slice(CH // 2, CH)]
+            pieces = [(block, slice(0, CH)) for block in range(BLOCKS - 1)]
+            pieces.extend([(BLOCKS - 1, half) for half in halves])
+            for n, (block, columns) in enumerate(pieces):
+                bank = banks.tile([P, BANK_F32], F32, tag="bank")
+                for g in range(TOKEN_PASSES):
+                    score_pass(bank, b, g, block, columns)
+                store_scores(bank, b, block, columns, by_vector=(n % 2 == 0))
 
         x_grouped_0 = transpose_x(0, 0)
         x_grouped_1 = transpose_x(0, 1)
-        quantise_x(0, 0, x_grouped_0)
+        quantise_x(0, 0, x_grouped_0, parts=2)
         quantise_x(0, 1, x_grouped_1)
         for b in range(BATCH):
             more = b + 1 < BATCH
@@ -170,10 +205,12 @@ def tile_transformer_block_pa_t_kernel(tc, x, w_qk_words, w_qk_scales, out):
             quantise_qk(b, 0, grouped_tiles)
             if more:
                 quantise_x(b + 1, 0, x_grouped_0)
-            grouped_tiles = project(b, 1)
             if more:
+                grouped_tiles = project(b, 1)
                 quantise_x(b + 1, 1, x_grouped_1)
-            quantise_qk(b, 1, grouped_tiles)
+                quantise_qk(b, 1, grouped_tiles)
+            else:
+                last_project(b, 1)
             if b > 0:
                 scores(b - 1)
-        scores(BATCH - 1)
+        last_scores(BATCH - 1)

@@ -22,6 +22,7 @@ TOKEN_PASSES = SEQ // K_PASS
 BLOCKS = CH // P
 PSUM_BANKS = 8
 BANK_F32 = 512
+WARM_MATMULS = 5
 
 FLOPS = 2 * BATCH * (2 * CH) * SEQ * CH + 2 * BATCH * CH * CH * SEQ
 
@@ -36,6 +37,7 @@ def tile_transformer_block_pa_t_kernel(tc, x, w_qk_words, w_qk_scales, out):
 
         batch_passes = [(b, g) for b in range(BATCH) for g in range(TOKEN_PASSES)]
         identity = keep.tile([P, P], F32)
+        warm = keep.tile([P, BANK_F32], BF16)
         w_codes = keep.tile([P, 2 * CH], U32, align_bytes=64)
         w_plane = keep.tile([P, 2 * CH], U8, align_bytes=64)
         x_sb = {}
@@ -54,6 +56,11 @@ def tile_transformer_block_pa_t_kernel(tc, x, w_qk_words, w_qk_scales, out):
             rows = x[b, g * K_PASS : (g + 1) * K_PASS, :].rearrange("(p j) c -> p j c", j=PACK)
             for j0 in range(0, PACK, 2):
                 nc.sync.dma_start(out=x_sb[b, g][:, j0 : j0 + 2], in_=rows[:, j0 : j0 + 2])
+
+        nc.vector.memset(warm[:], 0.0)
+        warm_bank = banks.tile([P, BANK_F32], F32, tag="bank")
+        for i in range(WARM_MATMULS):
+            nc.tensor.matmul(warm_bank[:], warm[:, :P], warm[:], start=True, stop=True)
 
         masks.make_identity(nc, identity[:])
         nc.vector.memset(w_plane[:].bitcast(I32), 0)

@@ -52,10 +52,11 @@ def tile_transformer_block_pa_t_kernel(tc, x, w_qk_words, w_qk_scales, out):
             qk_codes[b, g] = keep.tile([P, 2 * CH], U32, name="qk_codes%d%d" % (b, g), align_bytes=64)
             qk_plane[b, g] = keep.tile([P, 2 * CH], U8, name="qk_plane%d%d" % (b, g), align_bytes=64)
 
-        def load_x(b, g):
+        def load_x(b, g, loads=1):
             rows = x[b, g * K_PASS : (g + 1) * K_PASS, :].rearrange("(p j) c -> p j c", j=PACK)
-            for j0 in range(0, PACK, 2):
-                nc.sync.dma_start(out=x_sb[b, g][:, j0 : j0 + 2], in_=rows[:, j0 : j0 + 2])
+            width = PACK // loads
+            for j0 in range(0, PACK, width):
+                nc.sync.dma_start(out=x_sb[b, g][:, j0 : j0 + width], in_=rows[:, j0 : j0 + width])
 
         nc.vector.memset(warm[:], 0.0)
         warm_bank = banks.tile([P, BANK_F32], F32, tag="bank")
@@ -64,7 +65,7 @@ def tile_transformer_block_pa_t_kernel(tc, x, w_qk_words, w_qk_scales, out):
 
         masks.make_identity(nc, identity[:])
         nc.vector.memset(w_plane[:].bitcast(I32), 0)
-        load_x(0, 0)
+        load_x(0, 0, loads=2)
         load_x(0, 1)
         for quadrant in range(4):
             nc.sync.dma_start(
@@ -166,7 +167,7 @@ def tile_transformer_block_pa_t_kernel(tc, x, w_qk_words, w_qk_scales, out):
 
         def store_scores(bank, b, block, columns, by_vector):
             width = columns.stop - columns.start
-            score_sb = stage.tile([P, CH], F32, tag="score_sb", bufs=2 * BLOCKS)
+            score_sb = stage.tile([P, CH], F32, tag="score_sb", bufs=3 * BLOCKS)
             if by_vector:
                 nc.vector.tensor_scalar_mul(
                     out=score_sb[:, :width], in0=bank[:, :width], scalar1=1.0 / math.sqrt(SEQ)
@@ -179,15 +180,11 @@ def tile_transformer_block_pa_t_kernel(tc, x, w_qk_words, w_qk_scales, out):
 
         def scores(b):
             columns = slice(0, CH)
-            score_banks = [
-                banks.tile([P, BANK_F32], F32, tag="bank", name="score_bank%d" % block)
-                for block in range(BLOCKS)
-            ]
-            for g in range(TOKEN_PASSES):
-                for block in range(BLOCKS):
-                    score_pass(score_banks[block], b, g, block, columns)
             for block in range(BLOCKS):
-                store_scores(score_banks[block], b, block, columns, by_vector=(block == BLOCKS - 1))
+                bank = banks.tile([P, BANK_F32], F32, tag="bank")
+                for g in range(TOKEN_PASSES):
+                    score_pass(bank, b, g, block, columns)
+                store_scores(bank, b, block, columns, by_vector=(block == BLOCKS - 1))
 
         def last_scores(b):
             halves = [slice(0, CH // 2), slice(CH // 2, CH)]

@@ -205,14 +205,14 @@ def tile_transformer_block_pa_t_kernel(tc, x, w_qk_words, w_qk_scales, out):
             grouped_tiles = project(b, 0)
             if more:
                 x_grouped_0 = transpose_x(b + 1, 0)
-                x_grouped_1 = transpose_x(b + 1, 1)
             quantise_qk(b, 0, grouped_tiles)
             if more:
                 quantise_x(b + 1, 0, x_grouped_0)
             if more:
                 grouped_tiles = project(b, 1)
-                quantise_x(b + 1, 1, x_grouped_1)
+                x_grouped_1 = transpose_x(b + 1, 1)
                 quantise_qk(b, 1, grouped_tiles)
+                quantise_x(b + 1, 1, x_grouped_1)
             else:
                 last_project(b, 1)
             if b > 0:

@@ -141,17 +141,6 @@ def tile_transformer_block_pa_t_kernel(tc, x, w_qk_words, w_qk_scales, out):
                     in_=grouped[:].rearrange("m i n t -> m (i n t)"),
                 )
 
-        def last_project(b, g):
-            quantise_qk(b, g, project_half(b, g, BLOCKS))
-            q_01 = stage.tile([P, 2, P, PACK], BF16, tag="by_scalar", align_bytes=64)
-            q_2 = stage.tile([P, 1, P, PACK], BF16, tag="by_vector", align_bytes=64)
-            q_3 = stage.tile([P, 1, P, PACK], BF16, tag="by_scalar", align_bytes=64)
-            project_block(b, g, 0, q_01[:, 0], nc.scalar.copy)
-            project_block(b, g, 2, q_2[:, 0], nc.vector.tensor_copy)
-            project_block(b, g, 1, q_01[:, 1], nc.scalar.copy)
-            project_block(b, g, 3, q_3[:, 0], nc.scalar.copy)
-            quantise_qk(b, g, [(0, q_01), (2, q_2), (3, q_3)])
-
         def score_pass(bank, b, g, block, columns):
             q_channels = slice(block * P, (block + 1) * P)
             k_channels = slice(CH + columns.start, CH + columns.stop)
@@ -178,23 +167,34 @@ def tile_transformer_block_pa_t_kernel(tc, x, w_qk_words, w_qk_scales, out):
                 out=out[b, block * P : (block + 1) * P, columns], in_=score_sb[:, :width]
             )
 
-        def scores(b):
-            columns = slice(0, CH)
-            for block in range(BLOCKS):
-                bank = banks.tile([P, BANK_F32], F32, tag="bank")
-                for g in range(TOKEN_PASSES):
-                    score_pass(bank, b, g, block, columns)
-                store_scores(bank, b, block, columns, by_vector=(block == BLOCKS - 1))
+        def score_block(b, block, columns, by_vector):
+            bank = banks.tile([P, BANK_F32], F32, tag="bank")
+            for g in range(TOKEN_PASSES):
+                score_pass(bank, b, g, block, columns)
+            store_scores(bank, b, block, columns, by_vector)
 
-        def last_scores(b):
-            halves = [slice(0, CH // 2), slice(CH // 2, CH)]
-            pieces = [(block, slice(0, CH)) for block in range(BLOCKS - 1)]
-            pieces.extend([(BLOCKS - 1, half) for half in halves])
-            for n, (block, columns) in enumerate(pieces):
-                bank = banks.tile([P, BANK_F32], F32, tag="bank")
-                for g in range(TOKEN_PASSES):
-                    score_pass(bank, b, g, block, columns)
-                store_scores(bank, b, block, columns, by_vector=(n % 2 == 0))
+        def scores(b):
+            for block in range(BLOCKS):
+                score_block(b, block, slice(0, CH), by_vector=(block == BLOCKS - 1 and b == 0))
+
+        def finish(b, g):
+            def q_block(block):
+                q_one = stage.tile([P, 1, P, PACK], BF16, tag="by_scalar", align_bytes=64)
+                project_block(b, g, block, q_one[:, 0], nc.scalar.copy)
+                quantise_qk(b, g, [(block, q_one)])
+
+            quantise_qk(b, g, project_half(b, g, BLOCKS))
+            q_block(0)
+            score_block(b - 1, 2, slice(0, CH), by_vector=False)
+            q_block(1)
+            score_block(b - 1, 3, slice(0, CH), by_vector=True)
+            q_block(2)
+            score_block(b, 0, slice(0, CH), by_vector=True)
+            q_block(3)
+            score_block(b, 1, slice(0, CH), by_vector=False)
+            for block in (2, 3):
+                score_block(b, block, slice(0, CH // 2), by_vector=False)
+                score_block(b, block, slice(CH // 2, CH), by_vector=True)
 
         x_grouped_0 = transpose_x(0, 0)
         x_grouped_1 = transpose_x(0, 1)
@@ -213,8 +213,9 @@ def tile_transformer_block_pa_t_kernel(tc, x, w_qk_words, w_qk_scales, out):
                 x_grouped_1 = transpose_x(b + 1, 1)
                 quantise_qk(b, 1, grouped_tiles)
                 quantise_x(b + 1, 1, x_grouped_1)
+                if b > 0:
+                    scores(b - 1)
             else:
-                last_project(b, 1)
-            if b > 0:
-                scores(b - 1)
-        last_scores(BATCH - 1)
+                for block in range(2):
+                    score_block(b - 1, block, slice(0, CH), by_vector=(block == 1))
+                finish(b, 1)

@@ -22,7 +22,8 @@ TOKEN_PASSES = SEQ // K_PASS
 BLOCKS = CH // P
 PSUM_BANKS = 8
 BANK_F32 = 512
-WARM_MATMULS = 5
+WARM_MATMULS = 8
+WARM_COLUMNS = 256
 
 FLOPS = 2 * BATCH * (2 * CH) * SEQ * CH + 2 * BATCH * CH * CH * SEQ
 
@@ -37,7 +38,7 @@ def tile_transformer_block_pa_t_kernel(tc, x, w_qk_words, w_qk_scales, out):
 
         batch_passes = [(b, g) for b in range(BATCH) for g in range(TOKEN_PASSES)]
         identity = keep.tile([P, P], F32)
-        warm = keep.tile([P, BANK_F32], BF16)
+        warm = keep.tile([P, WARM_COLUMNS], BF16)
         w_codes = keep.tile([P, 2 * CH], U32, align_bytes=64)
         w_plane = keep.tile([P, 2 * CH], U8, align_bytes=64)
         x_sb = {}
@@ -61,7 +62,7 @@ def tile_transformer_block_pa_t_kernel(tc, x, w_qk_words, w_qk_scales, out):
         nc.vector.memset(warm[:], 0.0)
         warm_bank = banks.tile([P, BANK_F32], F32, tag="bank")
         for i in range(WARM_MATMULS):
-            nc.tensor.matmul(warm_bank[:], warm[:, :P], warm[:], start=True, stop=True)
+            nc.tensor.matmul(warm_bank[:, :WARM_COLUMNS], warm[:, :P], warm[:], start=True, stop=True)
 
         masks.make_identity(nc, identity[:])
         nc.vector.memset(w_plane[:].bitcast(I32), 0)
@@ -121,25 +122,28 @@ def tile_transformer_block_pa_t_kernel(tc, x, w_qk_words, w_qk_scales, out):
                 )
             copy_out(out=side_by_side, in_=bank[:].rearrange("m t n -> m n t"))
 
-        def project_half(b, g, first_block):
-            by_scalar = stage.tile([P, 2, P, PACK], BF16, tag="by_scalar", align_bytes=64)
-            by_vector = stage.tile([P, 2, P, PACK], BF16, tag="by_vector", align_bytes=64)
-            for i in range(2):
-                project_block(b, g, first_block + i, by_scalar[:, i], nc.scalar.copy)
-                project_block(b, g, first_block + 2 + i, by_vector[:, i], nc.vector.tensor_copy)
-            return [(first_block, by_scalar), (first_block + 2, by_vector)]
+        def project_half(b, g, first_block, last_by_vector=True):
+            grouped = stage.tile([P, BLOCKS, P, PACK], BF16, tag="grouped", align_bytes=64)
+            for i in range(BLOCKS):
+                by_vector = i % 2 == 1 and (i < BLOCKS - 1 or last_by_vector)
+                copy_out = nc.vector.tensor_copy if by_vector else nc.scalar.copy
+                project_block(b, g, first_block + i, grouped[:, i], copy_out)
+            return [(first_block, grouped)]
 
         def project(b, g):
-            return project_half(b, g, 0) + project_half(b, g, BLOCKS)
+            last_by_vector = g > 0 or b == BATCH - 1
+            return project_half(b, g, 0) + project_half(b, g, BLOCKS, last_by_vector)
 
-        def quantise_qk(b, g, grouped_tiles):
+        def quantise_qk(b, g, grouped_tiles, calls=1):
             for first_block, grouped in grouped_tiles:
-                channels = slice(first_block * P, (first_block + grouped.shape[1]) * P)
-                nc.vector.quantize_mx(
-                    out=qk_codes[b, g][:, channels].bitcast(FP8X4),
-                    scales=qk_plane[b, g][:, channels],
-                    in_=grouped[:].rearrange("m i n t -> m (i n t)"),
-                )
+                width = grouped.shape[1] // calls
+                for i in range(0, grouped.shape[1], width):
+                    channels = slice((first_block + i) * P, (first_block + i + width) * P)
+                    nc.vector.quantize_mx(
+                        out=qk_codes[b, g][:, channels].bitcast(FP8X4),
+                        scales=qk_plane[b, g][:, channels],
+                        in_=grouped[:, i : i + width].rearrange("m i n t -> m (i n t)"),
+                    )
 
         def score_pass(bank, b, g, block, columns):
             q_channels = slice(block * P, (block + 1) * P)
@@ -175,15 +179,15 @@ def tile_transformer_block_pa_t_kernel(tc, x, w_qk_words, w_qk_scales, out):
 
         def scores(b):
             for block in range(BLOCKS):
-                score_block(b, block, slice(0, CH), by_vector=(block == BLOCKS - 1 and b == 0))
+                score_block(b, block, slice(0, CH), by_vector=(block >= BLOCKS // 2))
 
         def finish(b, g):
             def q_block(block):
-                q_one = stage.tile([P, 1, P, PACK], BF16, tag="by_scalar", align_bytes=64)
+                q_one = stage.tile([P, 1, P, PACK], BF16, tag="grouped", align_bytes=64)
                 project_block(b, g, block, q_one[:, 0], nc.scalar.copy)
                 quantise_qk(b, g, [(block, q_one)])
 
-            quantise_qk(b, g, project_half(b, g, BLOCKS))
+            quantise_qk(b, g, project_half(b, g, BLOCKS), calls=2)
             q_block(0)
             score_block(b - 1, 2, slice(0, CH), by_vector=False)
             q_block(1)
@@ -217,5 +221,5 @@ def tile_transformer_block_pa_t_kernel(tc, x, w_qk_words, w_qk_scales, out):
                     scores(b - 1)
             else:
                 for block in range(2):
-                    score_block(b - 1, block, slice(0, CH), by_vector=(block == 1))
+                    score_block(b - 1, block, slice(0, CH), by_vector=False)
                 finish(b, 1)

@@ -60,9 +60,15 @@ def tile_transformer_block_pa_t_kernel(tc, x, w_qk_words, w_qk_scales, out):
                 nc.sync.dma_start(out=x_sb[b, g][:, j0 : j0 + width], in_=rows[:, j0 : j0 + width])
 
         nc.vector.memset(warm[:], 0.0)
-        warm_bank = banks.tile([P, BANK_F32], F32, tag="bank")
-        for i in range(WARM_MATMULS):
-            nc.tensor.matmul(warm_bank[:, :WARM_COLUMNS], warm[:, :P], warm[:], start=True, stop=True)
+
+        def keep_warm(matmuls):
+            warm_bank = banks.tile([P, BANK_F32], F32, tag="bank")
+            for i in range(matmuls):
+                nc.tensor.matmul(
+                    warm_bank[:, :WARM_COLUMNS], warm[:, :P], warm[:], start=True, stop=True
+                )
+
+        keep_warm(WARM_MATMULS)
 
         masks.make_identity(nc, identity[:])
         nc.vector.memset(w_plane[:].bitcast(I32), 0)
@@ -201,6 +207,7 @@ def tile_transformer_block_pa_t_kernel(tc, x, w_qk_words, w_qk_scales, out):
                 score_block(b, block, slice(CH // 2, CH), by_vector=True)
 
         x_grouped_0 = transpose_x(0, 0)
+        keep_warm(4)
         x_grouped_1 = transpose_x(0, 1)
         quantise_x(0, 0, x_grouped_0, parts=2)
         quantise_x(0, 1, x_grouped_1)

import math
from contextlib import ExitStack

import concourse.masks as masks
import concourse.mybir as mybir

F32 = mybir.dt.float32
BF16 = mybir.dt.bfloat16
I32 = mybir.dt.int32
U32 = mybir.dt.uint32
U8 = mybir.dt.uint8
FP8X4 = mybir.dt.float8_e4m3fn_x4

P = 128
PACK = 4
K_PASS = P * PACK

BATCH = 4
SEQ = 1024
CH = 512
TOKEN_PASSES = SEQ // K_PASS
BLOCKS = CH // P
PSUM_BANKS = 8
BANK_F32 = 512
WARM_MATMULS = 8
WARM_COLUMNS = 256

FLOPS = 2 * BATCH * (2 * CH) * SEQ * CH + 2 * BATCH * CH * CH * SEQ


def tile_transformer_block_pa_t_kernel(tc, x, w_qk_words, w_qk_scales, out):
    nc = tc.nc
    with ExitStack() as ctx:
        keep = ctx.enter_context(tc.tile_pool(name="keep", bufs=1))
        stage = ctx.enter_context(tc.tile_pool(name="stage", bufs=4))
        banks = ctx.enter_context(tc.psum_pool(name="banks", bufs=PSUM_BANKS))
        ctx.enter_context(tc.manual_schedule())

        batch_passes = [(b, g) for b in range(BATCH) for g in range(TOKEN_PASSES)]
        identity = keep.tile([P, P], F32)
        warm = keep.tile([P, WARM_COLUMNS], BF16)
        w_codes = keep.tile([P, 2 * CH], U32, align_bytes=64)
        w_plane = keep.tile([P, 2 * CH], U8, align_bytes=64)
        x_sb = {}
        x_codes = {}
        x_plane = {}
        qk_codes = {}
        qk_plane = {}
        for b, g in batch_passes:
            x_sb[b, g] = keep.tile([P, PACK, CH], BF16, name="x_sb%d%d" % (b, g))
            x_codes[b, g] = keep.tile([P, K_PASS], U32, name="x_codes%d%d" % (b, g), align_bytes=64)
            x_plane[b, g] = keep.tile([P, K_PASS], U8, name="x_plane%d%d" % (b, g), align_bytes=64)
            qk_codes[b, g] = keep.tile([P, 2 * CH], U32, name="qk_codes%d%d" % (b, g), align_bytes=64)
            qk_plane[b, g] = keep.tile([P, 2 * CH], U8, name="qk_plane%d%d" % (b, g), align_bytes=64)

        def load_x(b, g, loads=1):
            rows = x[b, g * K_PASS : (g + 1) * K_PASS, :].rearrange("(p j) c -> p j c", j=PACK)
            width = PACK // loads
            for j0 in range(0, PACK, width):
                nc.sync.dma_start(out=x_sb[b, g][:, j0 : j0 + width], in_=rows[:, j0 : j0 + width])

        nc.vector.memset(warm[:], 0.0)

        def keep_warm(matmuls):
            warm_bank = banks.tile([P, BANK_F32], F32, tag="bank")
            for i in range(matmuls):
                nc.tensor.matmul(
                    warm_bank[:, :WARM_COLUMNS], warm[:, :P], warm[:], start=True, stop=True
                )

        keep_warm(WARM_MATMULS)

        masks.make_identity(nc, identity[:])
        nc.vector.memset(w_plane[:].bitcast(I32), 0)
        load_x(0, 0, loads=2)
        load_x(0, 1)
        for quadrant in range(4):
            nc.sync.dma_start(
                out=w_plane[32 * quadrant : 32 * quadrant + 4, :].bitcast(I32),
                in_=w_qk_scales[0, 4 * quadrant : 4 * quadrant + 4, :].bitcast(I32),
            )
        w_words = w_qk_words[0].rearrange("p n t -> p (n t)").bitcast(I32)
        for channels in (slice(0, CH), slice(CH, 2 * CH)):
            nc.sync.dma_start(out=w_codes[:, channels].bitcast(I32), in_=w_words[:, channels])
        for b, g in batch_passes[TOKEN_PASSES:]:
            load_x(b, g)

        def transpose_x(b, g):
            x_grouped = stage.tile([P, PACK, P, PACK], BF16, tag="x_grouped", align_bytes=64)
            x_pairs = x_sb[b, g][:].bitcast(F32)
            grouped_pairs = x_grouped[:].bitcast(F32)
            for j0 in range(0, PACK, 2):
                bank = banks.tile([P, 2, 2, P], F32, tag="bank")
                for jj in range(2):
                    for u in range(2):
                        nc.tensor.transpose(
                            bank[:, jj, u, :], x_pairs[:, j0 + jj, u : CH // 2 : 2], identity[:]
                        )
                nc.scalar.copy(
                    out=grouped_pairs[:, j0 : j0 + 2],
                    in_=bank[:].rearrange("q jj u m -> q jj m u"),
                )
            return x_grouped

        def quantise_x(b, g, x_grouped, parts=1):
            width = PACK // parts
            for j0 in range(0, PACK, width):
                columns = slice(j0 * P, (j0 + width) * P)
                nc.vector.quantize_mx(
                    out=x_codes[b, g][:, columns].bitcast(FP8X4),
                    scales=x_plane[b, g][:, columns],
                    in_=x_grouped[:, j0 : j0 + width].rearrange("q j m t -> q (j m t)"),
                )

        def project_block(b, g, block, side_by_side, copy_out):
            channels = slice(block * P, (block + 1) * P)
            bank = banks.tile([P, PACK, P], F32, tag="bank")
            for t in range(PACK):
                tokens = slice(t * P, (t + 1) * P)
                nc.tensor.matmul_mx(
                    out=bank[:, t, :],
                    lhsT=x_codes[b, g][:, tokens].bitcast(FP8X4),
                    lhsT_scale=x_plane[b, g][:, tokens],
                    rhs=w_codes[:, channels].bitcast(FP8X4),
                    rhs_scale=w_plane[:, channels],
                    start=True,
                    stop=True,
                )
            copy_out(out=side_by_side, in_=bank[:].rearrange("m t n -> m n t"))

        def project_half(b, g, first_block, last_by_vector=True):
            grouped = stage.tile([P, BLOCKS, P, PACK], BF16, tag="grouped", align_bytes=64)
            for i in range(BLOCKS):
                by_vector = i % 2 == 1 and (i < BLOCKS - 1 or last_by_vector)
                copy_out = nc.vector.tensor_copy if by_vector else nc.scalar.copy
                project_block(b, g, first_block + i, grouped[:, i], copy_out)
            return [(first_block, grouped)]

        def project(b, g):
            last_by_vector = g > 0 or b == BATCH - 1
            return project_half(b, g, 0) + project_half(b, g, BLOCKS, last_by_vector)

        def quantise_qk(b, g, grouped_tiles, calls=1):
            for first_block, grouped in grouped_tiles:
                width = grouped.shape[1] // calls
                for i in range(0, grouped.shape[1], width):
                    channels = slice((first_block + i) * P, (first_block + i + width) * P)
                    nc.vector.quantize_mx(
                        out=qk_codes[b, g][:, channels].bitcast(FP8X4),
                        scales=qk_plane[b, g][:, channels],
                        in_=grouped[:, i : i + width].rearrange("m i n t -> m (i n t)"),
                    )

        def score_pass(bank, b, g, block, columns):
            q_channels = slice(block * P, (block + 1) * P)
            k_channels = slice(CH + columns.start, CH + columns.stop)
            nc.tensor.matmul_mx(
                out=bank[:, : columns.stop - columns.start],
                lhsT=qk_codes[b, g][:, q_channels].bitcast(FP8X4),
                lhsT_scale=qk_plane[b, g][:, q_channels],
                rhs=qk_codes[b, g][:, k_channels].bitcast(FP8X4),
                rhs_scale=qk_plane[b, g][:, k_channels],
                start=(g == 0),
                stop=(g == TOKEN_PASSES - 1),
            )

        def store_scores(bank, b, block, columns, by_vector):
            width = columns.stop - columns.start
            score_sb = stage.tile([P, CH], F32, tag="score_sb", bufs=3 * BLOCKS)
            if by_vector:
                nc.vector.tensor_scalar_mul(
                    out=score_sb[:, :width], in0=bank[:, :width], scalar1=1.0 / math.sqrt(SEQ)
                )
            else:
                nc.scalar.mul(out=score_sb[:, :width], in_=bank[:, :width], mul=1.0 / math.sqrt(SEQ))
            nc.sync.dma_start(
                out=out[b, block * P : (block + 1) * P, columns], in_=score_sb[:, :width]
            )

        def score_block(b, block, columns, by_vector):
            bank = banks.tile([P, BANK_F32], F32, tag="bank")
            for g in range(TOKEN_PASSES):
                score_pass(bank, b, g, block, columns)
            store_scores(bank, b, block, columns, by_vector)

        def scores(b):
            for block in range(BLOCKS):
                score_block(b, block, slice(0, CH), by_vector=(block >= BLOCKS // 2))

        def finish(b, g):
            def q_block(block):
                q_one = stage.tile([P, 1, P, PACK], BF16, tag="grouped", align_bytes=64)
                project_block(b, g, block, q_one[:, 0], nc.scalar.copy)
                quantise_qk(b, g, [(block, q_one)])

            quantise_qk(b, g, project_half(b, g, BLOCKS), calls=2)
            q_block(0)
            score_block(b - 1, 2, slice(0, CH), by_vector=False)
            q_block(1)
            score_block(b - 1, 3, slice(0, CH), by_vector=True)
            q_block(2)
            score_block(b, 0, slice(0, CH), by_vector=True)
            q_block(3)
            score_block(b, 1, slice(0, CH), by_vector=False)
            for block in (2, 3):
                score_block(b, block, slice(0, CH // 2), by_vector=False)
                score_block(b, block, slice(CH // 2, CH), by_vector=True)

        x_grouped_0 = transpose_x(0, 0)
        keep_warm(4)
        x_grouped_1 = transpose_x(0, 1)
        quantise_x(0, 0, x_grouped_0, parts=2)
        quantise_x(0, 1, x_grouped_1)
        for b in range(BATCH):
            more = b + 1 < BATCH
            grouped_tiles = project(b, 0)
            if more:
                x_grouped_0 = transpose_x(b + 1, 0)
            quantise_qk(b, 0, grouped_tiles)
            if more:
                quantise_x(b + 1, 0, x_grouped_0)
            if more:
                grouped_tiles = project(b, 1)
                x_grouped_1 = transpose_x(b + 1, 1)
                quantise_qk(b, 1, grouped_tiles)
                quantise_x(b + 1, 1, x_grouped_1)
                if b > 0:
                    scores(b - 1)
            else:
                for block in range(2):
                    score_block(b - 1, block, slice(0, CH), by_vector=False)
                finish(b, 1)
